import numpy as np
import ml_dtypes


def mxq(x, axis, fmt="e4m3"):
    dtype, down = {"e4m3": (ml_dtypes.float8_e4m3fn, 7), "e5m2": (ml_dtypes.float8_e5m2, 14)}[fmt]
    v = np.moveaxis(np.asarray(x, np.float32).astype(ml_dtypes.bfloat16).astype(np.float64), axis, -1)
    blocks = v.reshape(v.shape[:-1] + (-1, 32))
    amax = np.abs(blocks).max(-1, keepdims=True)
    byte = np.maximum(np.where(amax > 0, np.frexp(amax)[1] - 1 + 127, 0) - down, 1)
    scale = np.exp2(byte - 127.0)
    codes = (blocks / scale).astype(np.float32).astype(dtype).astype(np.float64)
    return np.moveaxis((codes * scale).reshape(v.shape), -1, axis)


WIDE = False


def mx_kscale(k):
    if not WIDE:
        return np.ones(k)
    levels = np.array([10, -10, 5, -5, 0])
    if k % 512:
        return np.exp2(np.random.permutation(np.resize(levels, k // 32))).repeat(32)
    a = np.empty((k // 512, 16))
    for p in range(k // 512):
        a[p, :8] = np.random.permutation(np.resize(levels, 8))
        for g in range(8):
            far = levels[np.abs(levels - a[p, g]) >= 10]
            a[p, g + 8] = far[np.random.randint(len(far))]
    return np.exp2(a.ravel()).repeat(32)


BF16 = ml_dtypes.bfloat16


def bf(x):
    return np.asarray(x, np.float32).astype(BF16)


def f64(x):
    return np.asarray(x).astype(np.float64)


B, STACK, TUBE, CH, IMG, PATCH, EMBED = 4, 16, 2, 1, 96, 16, 1024
GH = IMG // PATCH
GW = IMG // PATCH
GD = STACK // TUBE
K = TUBE * CH * PATCH * PATCH


def _sincos_1d(dim, pos):
    omega = 1.0 / (10000.0 ** (np.arange(dim // 2, dtype=np.float64) / (dim / 2.0)))
    out = pos[:, None].astype(np.float64) * omega[None, :]
    return np.concatenate([np.sin(out), np.cos(out)], axis=1)


def get_3d_sincos_pos_embed(grid_h, grid_w, grid_depth, embed_dim):
    dim_t = embed_dim // 4
    dim_s = embed_dim - dim_t
    emb_t = _sincos_1d(dim_t, np.arange(grid_depth))
    emb_h = _sincos_1d(dim_s // 2, np.arange(grid_h))
    emb_w = _sincos_1d(dim_s - dim_s // 2, np.arange(grid_w))
    emb_hw = np.concatenate([np.repeat(emb_h, grid_w, axis=0), np.tile(emb_w, (grid_h, 1))], axis=1)
    ns = grid_h * grid_w
    return np.concatenate([np.repeat(emb_t, ns, axis=0), np.tile(emb_hw, (grid_depth, 1))], axis=1)


def setup_inputs():
    s = mx_kscale(K)
    sv = s.reshape(TUBE, CH, PATCH, PATCH)[:, :, None, :, None, :]
    video = np.random.standard_normal((B, GD, TUBE, CH, GH, PATCH, GW, PATCH)) * sv
    return {"video": bf(video.reshape(B, STACK, CH, IMG, IMG)),
            "W": bf(np.random.standard_normal((EMBED, K)) / np.sqrt(K) / s[None, :]),
            "b": bf(np.random.standard_normal(EMBED) * 0.3),
            "pos_embed": bf(get_3d_sincos_pos_embed(GH, GW, GD, EMBED)[None])}


def core(video, W, b, pos_embed):
    video = f64(video)
    B_, T, C, H, W_ = video.shape
    p = PATCH
    gh, gw = H // p, W_ // p
    ns = gh * gw
    x = video.reshape(B_ * T, C, gh, p, gw, p)
    x = x.transpose(0, 2, 4, 1, 3, 5)
    x = x.reshape(B_, T, ns, C * p * p)
    x = x.reshape(B_, GD, TUBE, ns, C * p * p)
    x = x.transpose(0, 1, 3, 2, 4)
    tubelets = x.reshape(B_, GD * ns, TUBE * C * p * p)
    tokens = (mxq(tubelets, 2, "e4m3") @ mxq(f64(W), 1, "e4m3").T) + f64(b) + f64(pos_embed)
    return tokens


def e4m3fn_bytes(y):
    return np.clip(np.asarray(y, np.float64), -448.0, 448.0).astype(np.float32).astype(ml_dtypes.float8_e4m3fn).view(np.uint8)


def reference(video, W, b, pos_embed):
    out = core(video, W, b, pos_embed)
    s = np.max(np.abs(out), axis=-1, keepdims=True) / 448.0
    return out, e4m3fn_bytes(out / s)

@@ -1,0 +1,456 @@
+from contextlib import ExitStack
+
+import concourse.mybir as mybir
+from concourse.masks import make_identity
+
+F32 = mybir.dt.float32
+BF16 = mybir.dt.bfloat16
+I32 = mybir.dt.int32
+U32 = mybir.dt.uint32
+U8 = mybir.dt.uint8
+FP8X4 = mybir.dt.float8_e4m3fn_x4
+FP8 = mybir.dt.float8_e4m3fn
+ALU = mybir.AluOpType
+ACT = mybir.ActivationFunctionType
+AX = mybir.AxisListType
+
+FLOPS = 2 * 1152 * 512 * 1024
+
+P = 128
+EMBED = 1024
+HALF = 512
+TILES = [(0, 0), (1, 0), (0, 1), (1, 1), (2, 0), (3, 0), (2, 1), (3, 1), (4, 2)]
+
+
+def tile_tubeletembedding_kernel(tc, video, W, b, pos_embed, out_0, out_1):
+    nc = tc.nc
+    with ExitStack() as ctx:
+        keep = ctx.enter_context(tc.tile_pool(name="keep", bufs=1))
+        xs = ctx.enter_context(tc.tile_pool(name="xs", bufs=9))
+        psum = ctx.enter_context(tc.psum_pool(name="psum", bufs=8))
+
+        brow = keep.tile([P, EMBED], BF16, name="brow")
+        zeros = keep.tile([P, 1], F32, name="zeros")
+        idn = keep.tile([P, P], F32, name="idn")
+        one = keep.tile([P, P], BF16, name="one")
+        wrm = keep.tile([P, 1], F32, name="wrm")
+        wraw = keep.tile([P, 8 * 512], BF16, name="wraw")
+        raws = []
+        relaid = []
+        for bp in range(2):
+            raw_t = keep.tile([P, 3072], BF16, name="raw%d" % bp)
+            rel_t = keep.tile([P, 1536], F32, name="rel%d" % bp)
+            raws.append(raw_t)
+            relaid.append(rel_t)
+        pos_sb = []
+        posb = []
+        for h in range(3):
+            pos_t = keep.tile([P, EMBED], BF16, name="pos%d" % h)
+            pos_sb.append(pos_t)
+            pt = keep.tile([P, EMBED], F32, name="posb%d" % h)
+            posb.append(pt)
+        bbt = keep.tile([P, EMBED], F32, name="bbt")
+        gw = keep.tile([P, 2048], F32, name="gw", align_bytes=64)
+        wc = keep.tile([P, EMBED], U32, name="wc", align_bytes=64)
+        ws = keep.tile([P, EMBED], U8, name="ws", align_bytes=64)
+        gv = keep.tile([P, 4 * 576], F32, name="gv", align_bytes=64)
+        g2 = keep.tile([P, 256], F32, name="g2", align_bytes=64)
+        vc = keep.tile([P, 1152], U32, name="vc", align_bytes=64)
+        vs = keep.tile([P, 1152], U8, name="vs", align_bytes=64)
+        amax = keep.tile([P, 16], F32, name="amax")
+        rcp = keep.tile([P, 16], F32, name="rcp")
+        fac = keep.tile([P, 16], F32, name="fac")
+        w_view = W.rearrange("(t p) k -> p t k", p=P)
+        w_words = wraw[:].bitcast(F32).rearrange("p (t w u) -> p t u w", t=8, w=128, u=2)
+        banks = {}
+        xts = {}
+        yts = {}
+        o8s = {}
+        queues = {"SP": nc.sync, "S": nc.scalar, "G": nc.gpsimd}
+
+        def copy_on(eng, out, in_):
+            if eng == "v":
+                nc.vector.tensor_copy(out=out, in_=in_)
+            elif eng == "g":
+                nc.gpsimd.tensor_copy(out=out, in_=in_)
+            else:
+                nc.scalar.copy(out=out, in_=in_)
+
+        def new_bank(key):
+            bank = psum.tile([P, HALF], F32, name="bank")
+            banks[key] = bank
+            return bank
+
+        def ms_brow(e):
+            nc.vector.memset(brow[:].bitcast(I32), 0)
+
+        def ms_zero(e):
+            nc.vector.memset(zeros[:], 0.0)
+
+        def ms_rel(bp, e):
+            if e == "v":
+                nc.vector.memset(relaid[bp][96:128, :], 0.0)
+            else:
+                nc.gpsimd.memset(relaid[bp][96:128, :], 0.0)
+
+        def ident():
+            make_identity(nc, idn[:])
+
+        def ones(e):
+            nc.gpsimd.memset(one[:], 1.0)
+
+        def warm():
+            nc.scalar.activation(out=wrm[:], in_=zeros[:], func=ACT.Identity)
+
+        def ld_b(q):
+            queues[q].dma_start(out=brow[0:1, :], in_=b.rearrange("(o e) -> o e", o=1))
+
+        def ld_w(q, h):
+            queues[q].dma_start(
+                out=wraw[:, h * 2048:(h + 1) * 2048].rearrange("p (t k) -> p t k", t=4),
+                in_=w_view[:, 4 * h:4 * h + 4, :])
+
+        def ld_v2(q, bp, ts):
+            src = video[2 * bp:2 * bp + 2, :, 0].rearrange(
+                "b (d t) (i y) x -> t (b d) i (y x)", t=2, y=16)
+            queues[q].dma_start(out=raws[bp][0:96, ts * 1536:(ts + 1) * 1536], in_=src[ts])
+
+        def ld_p(q, t):
+            if t < 2:
+                queues[q].dma_start(out=pos_sb[t][:], in_=pos_embed[0, t * P:(t + 1) * P, :])
+            else:
+                for bb in range(4):
+                    queues[q].dma_start(out=pos_sb[2][bb:128:4, :], in_=pos_embed[0, 256:288, :])
+
+        def dm(k):
+            if "dm" not in banks:
+                new_bank("dm")
+            nc.tensor.matmul(out=banks["dm"][:, 0:P], lhsT=idn[:], rhs=idn[:], start=True, stop=True)
+
+        def tw(tp):
+            bank = new_bank(("w", tp))
+            for t in range(2):
+                for u in range(2):
+                    s = 2 * t + u
+                    nc.tensor.transpose(out=bank[:, s * P:(s + 1) * P],
+                                        in_=w_words[:, 2 * tp + t, u, :], identity=idn[:])
+
+        def cw(tp, e):
+            copy_on(e, gw[:, tp * 512:(tp + 1) * 512].rearrange("p (t e u) -> p t e u", t=2, u=2),
+                    banks[("w", tp)][:].rearrange("p (t u e) -> p t e u", t=2, u=2))
+
+        def qw(h):
+            nc.vector.quantize_mx(out=wc[:, h * HALF:(h + 1) * HALF].bitcast(FP8X4),
+                                  scales=ws[:, h * HALF:(h + 1) * HALF],
+                                  in_=gw[:, h * 1024:(h + 1) * 1024].bitcast(BF16))
+
+        def rl(bp, j0, j1, e):
+            src = raws[bp][0:96, :].bitcast(F32).rearrange(
+                "p (r j q u) -> p j u r q", r=32, j=6, q=4, u=2)
+            dst = relaid[bp][0:96, :].rearrange("p (j u r q) -> p j u r q", j=6, u=2, r=32, q=4)
+            if j1 - j0 == 1:
+                copy_on(e, dst[:, j0], src[:, j0])
+            else:
+                copy_on(e, dst[:, j0:j1], src[:, j0:j1])
+
+        def tv(bp, jp):
+            bank = new_bank(("v", bp, jp))
+            for s in range(4):
+                c = 4 * jp + s
+                nc.tensor.transpose(out=bank[:, s * P:(s + 1) * P],
+                                    in_=relaid[bp][:, c * P:(c + 1) * P], identity=idn[:])
+
+        def cv(bp, jp, e):
+            dst = gv[:, bp * 1152:(bp + 1) * 1152].rearrange(
+                "p (c w) -> p c w", w=12)[:, :, 4 * jp:4 * jp + 4]
+            src = banks[("v", bp, jp)][:].rearrange("p (s c) -> p c s", s=4)[:, 0:96, :]
+            copy_on(e, dst, src)
+
+        def qv(bb):
+            nc.vector.quantize_mx(out=vc[:, bb * 256:(bb + 1) * 256].bitcast(FP8X4),
+                                  scales=vs[:, bb * 256:(bb + 1) * 256],
+                                  in_=gv[:, bb * 576:bb * 576 + 512].bitcast(BF16))
+
+        def r2c():
+            nc.vector.tensor_copy(
+                out=g2[:].rearrange("p (n b w) -> p b n w", b=4, w=2),
+                in_=gv[:].rearrange("p (b x) -> p b x", b=4)[:, :, 512:576].rearrange(
+                    "p b (n w) -> p b n w", w=2))
+
+        def r2q():
+            nc.vector.quantize_mx(out=vc[:, 1024:1152].bitcast(FP8X4), scales=vs[:, 1024:1152],
+                                  in_=g2[:].bitcast(BF16))
+
+        def pb():
+            for h in range(2):
+                bank = new_bank(("b", h))
+                nc.tensor.matmul(out=bank[:], lhsT=one[:], rhs=brow[:, h * HALF:(h + 1) * HALF],
+                                 start=True, stop=True)
+
+        def bbc(h):
+            nc.scalar.copy(out=bbt[:, h * HALF:(h + 1) * HALF], in_=banks[("b", h)][:])
+
+        def pp(t, h, e):
+            sl = slice(h * HALF, (h + 1) * HALF)
+            if e == "v":
+                nc.vector.tensor_tensor(out=posb[t][:, sl], in0=banks[("b", h)][:], in1=pos_sb[t][:, sl],
+                                        op=ALU.add)
+            else:
+                nc.gpsimd.tensor_tensor(out=posb[t][:, sl], in0=pos_sb[t][:, sl], in1=bbt[:, sl],
+                                        op=ALU.add)
+
+        def x_of(i):
+            if i not in xts:
+                x_t = xs.tile([P, EMBED], F32, name="x")
+                xts[i] = x_t
+            return xts[i]
+
+        def mm(i, n):
+            bb, h = TILES[i]
+            c0 = 1024 if h == 2 else (2 * bb + h) * P
+            acc = new_bank(("a", i, n))
+            nc.tensor.matmul_mx(out=acc[:],
+                                lhsT=vc[:, c0:c0 + P].bitcast(FP8X4), lhsT_scale=vs[:, c0:c0 + P],
+                                rhs=wc[:, n * HALF:(n + 1) * HALF].bitcast(FP8X4),
+                                rhs_scale=ws[:, n * HALF:(n + 1) * HALF],
+                                start=True, stop=True)
+
+        def av(i, n):
+            sl = slice(n * HALF, (n + 1) * HALF)
+            nc.vector.tensor_tensor(out=x_of(i)[:, sl], in0=banks[("a", i, n)][:],
+                                    in1=posb[TILES[i][1]][:, sl], op=ALU.add)
+
+        def ev(i, n):
+            y_t = xs.tile([P, HALF], F32, name="y")
+            yts[(i, n)] = y_t
+            nc.scalar.copy(out=y_t[:], in_=banks[("a", i, n)][:])
+
+        def ga(i, n):
+            sl = slice(n * HALF, (n + 1) * HALF)
+            nc.gpsimd.tensor_tensor(out=x_of(i)[:, sl], in0=yts[(i, n)][:],
+                                    in1=posb[TILES[i][1]][:, sl], op=ALU.add)
+
+        def sx(i, n):
+            bb, h = TILES[i]
+            sl = slice(n * HALF, (n + 1) * HALF)
+            if h == 2:
+                nc.sync.dma_start(out=out_0[:, 256:288, sl].rearrange("b n e -> n b e"), in_=xts[i][:, sl])
+            else:
+                nc.sync.dma_start(out=out_0[bb, h * P:(h + 1) * P, sl], in_=xts[i][:, sl])
+
+        def rd(i):
+            nc.vector.tensor_reduce(out=amax[:, i:i + 1], in_=xts[i][:], axis=AX.X, op=ALU.max,
+                                    apply_absolute_value=True)
+
+        def rc(i):
+            nc.vector.reciprocal(out=rcp[:, i:i + 1], in_=amax[:, i:i + 1])
+
+        def fm(i, e):
+            if e == "v":
+                nc.vector.tensor_scalar(out=fac[:, i:i + 1], in0=rcp[:, i:i + 1], scalar1=448.0,
+                                        scalar2=None, op0=ALU.mult)
+            else:
+                nc.scalar.activation(out=fac[:, i:i + 1], in_=rcp[:, i:i + 1], func=ACT.Identity,
+                                     scale=448.0)
+
+        def ct(i, e, lo, hi):
+            if i not in o8s:
+                o_t = xs.tile([P, EMBED], FP8, name="o8")
+                o8s[i] = o_t
+            if e == "v":
+                nc.vector.tensor_scalar(out=o8s[i][:, lo:hi], in0=xts[i][:, lo:hi],
+                                        scalar1=fac[:, i:i + 1], scalar2=None, op0=ALU.mult,
+                                        saturate=False)
+            else:
+                nc.scalar.activation(out=o8s[i][:, lo:hi], in_=xts[i][:, lo:hi], func=ACT.Identity,
+                                     scale=fac[:, i:i + 1], bias=zeros[:, 0:1], saturate=False)
+
+        def s8(i):
+            bb, h = TILES[i]
+            if h == 2:
+                dst = out_1[:, 256:288, :].rearrange("b n e -> n b e")
+            else:
+                dst = out_1[bb, h * P:(h + 1) * P, :]
+            nc.sync.dma_start(out=dst, in_=o8s[i][:].bitcast(U8))
+
+        ms_brow("v")
+        ms_zero("v")
+        ms_rel(0, "v")
+        ident()
+        ones("g")
+        ld_w("SP", 0)
+        ld_v2("SP", 0, 0)
+        ld_v2("SP", 0, 1)
+        ld_w("SP", 1)
+        ld_b("SP")
+        warm()
+        ld_p("SP", 0)
+        ld_p("SP", 1)
+        ld_v2("SP", 1, 0)
+        ld_v2("SP", 1, 1)
+        ms_rel(1, "g")
+        ld_p("SP", 2)
+        with tc.manual_schedule():
+            dm(0)
+            dm(1)
+            dm(2)
+            dm(3)
+            dm(4)
+            tw(0)
+            tw(1)
+            dm(5)
+            pb()
+            dm(6)
+            cw(0, "s")
+            cw(1, "s")
+            rl(0, 0, 2, "v")
+            rl(0, 2, 4, "v")
+            rl(0, 4, 5, "s")
+            rl(0, 5, 6, "s")
+            qw(0)
+            tv(0, 0)
+            tv(0, 1)
+            dm(7)
+            tv(0, 2)
+            tw(2)
+            dm(8)
+            tw(3)
+            cv(0, 0, "s")
+            cv(0, 1, "s")
+            cv(0, 2, "s")
+            pp(0, 0, "v")
+            pp(1, 0, "v")
+            bbc(1)
+            pp(0, 1, "g")
+            qv(0)
+            qv(1)
+            mm(0, 0)
+            mm(1, 0)
+            mm(2, 0)
+            mm(3, 0)
+            cw(2, "s")
+            cw(3, "s")
+            av(0, 0)
+            sx(0, 0)
+            pp(1, 1, "g")
+            rl(1, 0, 1, "s")
+            rl(1, 1, 2, "s")
+            rl(1, 2, 3, "s")
+            rl(1, 3, 4, "s")
+            rl(1, 4, 5, "s")
+            rl(1, 5, 6, "s")
+            qw(1)
+            av(1, 0)
+            sx(1, 0)
+            mm(0, 1)
+            mm(1, 1)
+            mm(2, 1)
+            mm(3, 1)
+            ev(1, 1)
+            ga(1, 1)
+            ev(2, 1)
+            ga(2, 1)
+            av(2, 0)
+            sx(2, 0)
+            av(3, 0)
+            sx(3, 0)
+            av(0, 1)
+            sx(0, 1)
+            pp(2, 0, "v")
+            tv(1, 0)
+            tv(1, 1)
+            tv(1, 2)
+            ev(3, 1)
+            ga(3, 1)
+            cv(1, 0, "s")
+            cv(1, 1, "s")
+            cv(1, 2, "s")
+            rd(0)
+            rc(0)
+            sx(1, 1)
+            qv(2)
+            qv(3)
+            fm(0, "s")
+            ct(0, "s", 0, 1024)
+            s8(0)
+            mm(4, 0)
+            mm(4, 1)
+            rd(1)
+            r2c()
+            rc(1)
+            sx(2, 1)
+            r2q()
+            fm(1, "s")
+            ev(4, 1)
+            ga(4, 1)
+            ct(1, "s", 0, 1024)
+            s8(1)
+            pp(2, 1, "g")
+            mm(5, 0)
+            mm(5, 1)
+            rd(2)
+            av(4, 0)
+            sx(4, 0)
+            rc(2)
+            sx(3, 1)
+            fm(2, "s")
+            ev(5, 1)
+            ga(5, 1)
+            ct(2, "s", 0, 1024)
+            s8(2)
+            mm(6, 0)
+            mm(6, 1)
+            rd(3)
+            av(5, 0)
+            sx(5, 0)
+            rc(3)
+            sx(4, 1)
+            fm(3, "s")
+            ev(6, 1)
+            ga(6, 1)
+            ct(3, "s", 0, 1024)
+            s8(3)
+            mm(7, 0)
+            mm(7, 1)
+            rd(4)
+            av(6, 0)
+            sx(6, 0)
+            rc(4)
+            sx(5, 1)
+            fm(4, "s")
+            ev(7, 1)
+            ga(7, 1)
+            ct(4, "s", 0, 1024)
+            s8(4)
+            mm(8, 0)
+            mm(8, 1)
+            rd(5)
+            av(7, 0)
+            sx(7, 0)
+            rc(5)
+            sx(6, 1)
+            fm(5, "s")
+            ev(8, 1)
+            ga(8, 1)
+            ct(5, "s", 0, 1024)
+            s8(5)
+            rd(6)
+            av(8, 0)
+            sx(8, 0)
+            rc(6)
+            sx(7, 1)
+            fm(6, "s")
+            ct(6, "s", 0, 1024)
+            s8(6)
+            rd(7)
+            rc(7)
+            sx(8, 1)
+            fm(7, "s")
+            ct(7, "s", 0, 1024)
+            s8(7)
+            rd(8)
+            rc(8)
+            fm(8, "v")
+            ct(8, "s", 0, 512)
+            ct(8, "v", 512, 1024)
+            s8(8)

@@ -34,6 +34,7 @@ def tile_tubeletembedding_kernel(tc, video, W, b, pos_embed, out_0, out_1):
         idn = keep.tile([P, P], F32, name="idn")
         one = keep.tile([P, P], BF16, name="one")
         wrm = keep.tile([P, 1], F32, name="wrm")
+        dmy = keep.tile([P, P], F32, name="dmy")
         wraw = keep.tile([P, 8 * 512], BF16, name="wraw")
         raws = []
         relaid = []
@@ -85,7 +86,13 @@ def tile_tubeletembedding_kernel(tc, video, W, b, pos_embed, out_0, out_1):
             nc.vector.memset(brow[:].bitcast(I32), 0)
 
         def ms_zero(e):
-            nc.vector.memset(zeros[:], 0.0)
+            if e == "v":
+                nc.vector.memset(zeros[:], 0.0)
+            else:
+                nc.gpsimd.memset(zeros[:], 0.0)
+
+        def ms_dmy():
+            nc.gpsimd.memset(dmy[:], 0.0)
 
         def ms_rel(bp, e):
             if e == "v":
@@ -97,7 +104,10 @@ def tile_tubeletembedding_kernel(tc, video, W, b, pos_embed, out_0, out_1):
             make_identity(nc, idn[:])
 
         def ones(e):
-            nc.gpsimd.memset(one[:], 1.0)
+            if e == "v":
+                nc.vector.memset(one[:], 1.0)
+            else:
+                nc.gpsimd.memset(one[:], 1.0)
 
         def warm():
             nc.scalar.activation(out=wrm[:], in_=zeros[:], func=ACT.Identity)
@@ -109,6 +119,11 @@ def tile_tubeletembedding_kernel(tc, video, W, b, pos_embed, out_0, out_1):
             queues[q].dma_start(
                 out=wraw[:, h * 2048:(h + 1) * 2048].rearrange("p (t k) -> p t k", t=4),
                 in_=w_view[:, 4 * h:4 * h + 4, :])
+
+        def ld_wq(q, tp):
+            queues[q].dma_start(
+                out=wraw[:, tp * 1024:(tp + 1) * 1024].rearrange("p (t k) -> p t k", t=2),
+                in_=w_view[:, 2 * tp:2 * tp + 2, :])
 
         def ld_v2(q, bp, ts):
             src = video[2 * bp:2 * bp + 2, :, 0].rearrange(
@@ -144,6 +159,11 @@ def tile_tubeletembedding_kernel(tc, video, W, b, pos_embed, out_0, out_1):
                                   scales=ws[:, h * HALF:(h + 1) * HALF],
                                   in_=gw[:, h * 1024:(h + 1) * 1024].bitcast(BF16))
 
+        def qwq(tp):
+            nc.vector.quantize_mx(out=wc[:, tp * 256:(tp + 1) * 256].bitcast(FP8X4),
+                                  scales=ws[:, tp * 256:(tp + 1) * 256],
+                                  in_=gw[:, tp * 512:(tp + 1) * 512].bitcast(BF16))
+
         def rl(bp, j0, j1, e):
             src = raws[bp][0:96, :].bitcast(F32).rearrange(
                 "p (r j q u) -> p j u r q", r=32, j=6, q=4, u=2)
@@ -171,11 +191,12 @@ def tile_tubeletembedding_kernel(tc, video, W, b, pos_embed, out_0, out_1):
                                   scales=vs[:, bb * 256:(bb + 1) * 256],
                                   in_=gv[:, bb * 576:bb * 576 + 512].bitcast(BF16))
 
-        def r2c():
-            nc.vector.tensor_copy(
-                out=g2[:].rearrange("p (n b w) -> p b n w", b=4, w=2),
-                in_=gv[:].rearrange("p (b x) -> p b x", b=4)[:, :, 512:576].rearrange(
-                    "p b (n w) -> p b n w", w=2))
+        def r2c(e):
+            copy_on(
+                e,
+                g2[:].rearrange("p (n b w) -> p n b w", b=4, w=2),
+                gv[:].rearrange("p (b x) -> p b x", b=4)[:, :, 512:576].rearrange(
+                    "p b (n w) -> p n b w", w=2))
 
         def r2q():
             nc.vector.quantize_mx(out=vc[:, 1024:1152].bitcast(FP8X4), scales=vs[:, 1024:1152],
@@ -198,6 +219,9 @@ def tile_tubeletembedding_kernel(tc, video, W, b, pos_embed, out_0, out_1):
             else:
                 nc.gpsimd.tensor_tensor(out=posb[t][:, sl], in0=pos_sb[t][:, sl], in1=bbt[:, sl],
                                         op=ALU.add)
+
+        def ppw(t):
+            nc.gpsimd.tensor_tensor(out=posb[t][:], in0=pos_sb[t][:], in1=bbt[:], op=ALU.add)
 
         def x_of(i):
             if i not in xts:
@@ -320,8 +344,6 @@ def tile_tubeletembedding_kernel(tc, video, W, b, pos_embed, out_0, out_1):
             cv(0, 2, "s")
             pp(0, 0, "v")
             pp(1, 0, "v")
-            bbc(1)
-            pp(0, 1, "g")
             qv(0)
             qv(1)
             mm(0, 0)
@@ -330,8 +352,11 @@ def tile_tubeletembedding_kernel(tc, video, W, b, pos_embed, out_0, out_1):
             mm(3, 0)
             cw(2, "s")
             cw(3, "s")
+            bbc(1)
             av(0, 0)
             sx(0, 0)
+            qw(1)
+            pp(0, 1, "g")
             pp(1, 1, "g")
             rl(1, 0, 1, "s")
             rl(1, 1, 2, "s")
@@ -339,47 +364,46 @@ def tile_tubeletembedding_kernel(tc, video, W, b, pos_embed, out_0, out_1):
             rl(1, 3, 4, "s")
             rl(1, 4, 5, "s")
             rl(1, 5, 6, "s")
-            qw(1)
             av(1, 0)
             sx(1, 0)
             mm(0, 1)
             mm(1, 1)
             mm(2, 1)
             mm(3, 1)
+            tv(1, 0)
+            tv(1, 1)
+            tv(1, 2)
             ev(1, 1)
             ga(1, 1)
-            ev(2, 1)
-            ga(2, 1)
             av(2, 0)
             sx(2, 0)
             av(3, 0)
             sx(3, 0)
             av(0, 1)
             sx(0, 1)
-            pp(2, 0, "v")
-            tv(1, 0)
-            tv(1, 1)
-            tv(1, 2)
-            ev(3, 1)
-            ga(3, 1)
             cv(1, 0, "s")
             cv(1, 1, "s")
             cv(1, 2, "s")
+            r2c("s")
             rd(0)
-            rc(0)
-            sx(1, 1)
             qv(2)
             qv(3)
+            r2q()
+            ev(2, 1)
+            ga(2, 1)
+            ev(3, 1)
+            ga(3, 1)
+            rc(0)
+            pp(2, 0, "v")
+            sx(1, 1)
             fm(0, "s")
             ct(0, "s", 0, 1024)
             s8(0)
             mm(4, 0)
             mm(4, 1)
             rd(1)
-            r2c()
             rc(1)
             sx(2, 1)
-            r2q()
             fm(1, "s")
             ev(4, 1)
             ga(4, 1)

@@ -389,32 +389,34 @@ def tile_tubeletembedding_kernel(tc, video, W, b, pos_embed, out_0, out_1):
             qv(2)
             qv(3)
             r2q()
-            ev(2, 1)
-            ga(2, 1)
-            ev(3, 1)
-            ga(3, 1)
             rc(0)
             pp(2, 0, "v")
             sx(1, 1)
             fm(0, "s")
+            ev(2, 1)
+            ga(2, 1)
+            ev(3, 1)
+            ga(3, 1)
             ct(0, "s", 0, 1024)
             s8(0)
             mm(4, 0)
             mm(4, 1)
             rd(1)
+            av(4, 0)
+            sx(4, 0)
             rc(1)
             sx(2, 1)
             fm(1, "s")
             ev(4, 1)
             ga(4, 1)
+            pp(2, 1, "g")
             ct(1, "s", 0, 1024)
             s8(1)
-            pp(2, 1, "g")
             mm(5, 0)
             mm(5, 1)
             rd(2)
-            av(4, 0)
-            sx(4, 0)
+            av(5, 0)
+            sx(5, 0)
             rc(2)
             sx(3, 1)
             fm(2, "s")
@@ -425,8 +427,8 @@ def tile_tubeletembedding_kernel(tc, video, W, b, pos_embed, out_0, out_1):
             mm(6, 0)
             mm(6, 1)
             rd(3)
-            av(5, 0)
-            sx(5, 0)
+            av(6, 0)
+            sx(6, 0)
             rc(3)
             sx(4, 1)
             fm(3, "s")
@@ -437,8 +439,8 @@ def tile_tubeletembedding_kernel(tc, video, W, b, pos_embed, out_0, out_1):
             mm(7, 0)
             mm(7, 1)
             rd(4)
-            av(6, 0)
-            sx(6, 0)
+            av(7, 0)
+            sx(7, 0)
             rc(4)
             sx(5, 1)
             fm(4, "s")
@@ -449,8 +451,8 @@ def tile_tubeletembedding_kernel(tc, video, W, b, pos_embed, out_0, out_1):
             mm(8, 0)
             mm(8, 1)
             rd(5)
-            av(7, 0)
-            sx(7, 0)
+            av(8, 0)
+            sx(8, 0)
             rc(5)
             sx(6, 1)
             fm(5, "s")
@@ -459,8 +461,6 @@ def tile_tubeletembedding_kernel(tc, video, W, b, pos_embed, out_0, out_1):
             ct(5, "s", 0, 1024)
             s8(5)
             rd(6)
-            av(8, 0)
-            sx(8, 0)
             rc(6)
             sx(7, 1)
             fm(6, "s")

@@ -83,7 +83,10 @@ def tile_tubeletembedding_kernel(tc, video, W, b, pos_embed, out_0, out_1):
             return bank
 
         def ms_brow(e):
-            nc.vector.memset(brow[:].bitcast(I32), 0)
+            if e == "v":
+                nc.vector.memset(brow[:].bitcast(I32), 0)
+            else:
+                nc.gpsimd.memset(brow[:].bitcast(F32), 0.0)
 
         def ms_zero(e):
             if e == "v":
@@ -117,8 +120,8 @@ def tile_tubeletembedding_kernel(tc, video, W, b, pos_embed, out_0, out_1):
 
         def ld_w(q, h):
             queues[q].dma_start(
-                out=wraw[:, h * 2048:(h + 1) * 2048].rearrange("p (t k) -> p t k", t=4),
-                in_=w_view[:, 4 * h:4 * h + 4, :])
+                out=wraw[:, h * 2048:(h + 1) * 2048],
+                in_=W[h * 512:(h + 1) * 512, :].rearrange("(p t) k -> p (t k)", t=4))
 
         def ld_wq(q, tp):
             queues[q].dma_start(
@@ -140,7 +143,7 @@ def tile_tubeletembedding_kernel(tc, video, W, b, pos_embed, out_0, out_1):
         def dm(k):
             if "dm" not in banks:
                 new_bank("dm")
-            nc.tensor.matmul(out=banks["dm"][:, 0:P], lhsT=idn[:], rhs=idn[:], start=True, stop=True)
+            nc.tensor.matmul(out=banks["dm"][:, 0:P], lhsT=dmy[:], rhs=dmy[:], start=True, stop=True)
 
         def tw(tp):
             bank = new_bank(("w", tp))
@@ -151,8 +154,9 @@ def tile_tubeletembedding_kernel(tc, video, W, b, pos_embed, out_0, out_1):
                                         in_=w_words[:, 2 * tp + t, u, :], identity=idn[:])
 
         def cw(tp, e):
-            copy_on(e, gw[:, tp * 512:(tp + 1) * 512].rearrange("p (t e u) -> p t e u", t=2, u=2),
-                    banks[("w", tp)][:].rearrange("p (t u e) -> p t e u", t=2, u=2))
+            h, a = divmod(tp, 2)
+            copy_on(e, gw[:, h * 1024:(h + 1) * 1024].rearrange("p (e a s) -> p a e s", a=2, s=4)[:, a],
+                    banks[("w", tp)][:].rearrange("p (s e) -> p e s", s=4))
 
         def qw(h):
             nc.vector.quantize_mx(out=wc[:, h * HALF:(h + 1) * HALF].bitcast(FP8X4),
@@ -297,22 +301,23 @@ def tile_tubeletembedding_kernel(tc, video, W, b, pos_embed, out_0, out_1):
                 dst = out_1[bb, h * P:(h + 1) * P, :]
             nc.sync.dma_start(out=dst, in_=o8s[i][:].bitcast(U8))
 
-        ms_brow("v")
+        ms_brow("g")
+        ms_dmy()
         ms_zero("v")
         ms_rel(0, "v")
         ident()
         ones("g")
         ld_w("SP", 0)
         ld_v2("SP", 0, 0)
+        ld_b("SP")
         ld_v2("SP", 0, 1)
         ld_w("SP", 1)
-        ld_b("SP")
         warm()
         ld_p("SP", 0)
         ld_p("SP", 1)
         ld_v2("SP", 1, 0)
         ld_v2("SP", 1, 1)
-        ms_rel(1, "g")
+        ms_rel(1, "v")
         ld_p("SP", 2)
         with tc.manual_schedule():
             dm(0)
@@ -475,6 +480,6 @@ def tile_tubeletembedding_kernel(tc, video, W, b, pos_embed, out_0, out_1):
             rd(8)
             rc(8)
             fm(8, "v")
-            ct(8, "s", 0, 512)
-            ct(8, "v", 512, 1024)
+            ct(8, "s", 0, 384)
+            ct(8, "v", 384, 1024)
             s8(8)

@@ -274,7 +274,10 @@ def tile_tubeletembedding_kernel(tc, video, W, b, pos_embed, out_0, out_1):
             nc.vector.reciprocal(out=rcp[:, i:i + 1], in_=amax[:, i:i + 1])
 
         def fm(i, e):
-            if e == "v":
+            if e == "g":
+                nc.gpsimd.tensor_scalar(out=fac[:, i:i + 1], in0=rcp[:, i:i + 1], scalar1=448.0,
+                                        scalar2=None, op0=ALU.mult)
+            elif e == "v":
                 nc.vector.tensor_scalar(out=fac[:, i:i + 1], in0=rcp[:, i:i + 1], scalar1=448.0,
                                         scalar2=None, op0=ALU.mult)
             else:
@@ -334,8 +337,7 @@ def tile_tubeletembedding_kernel(tc, video, W, b, pos_embed, out_0, out_1):
             cw(1, "s")
             rl(0, 0, 2, "v")
             rl(0, 2, 4, "v")
-            rl(0, 4, 5, "s")
-            rl(0, 5, 6, "s")
+            rl(0, 4, 6, "s")
             qw(0)
             tv(0, 0)
             tv(0, 1)
@@ -363,12 +365,9 @@ def tile_tubeletembedding_kernel(tc, video, W, b, pos_embed, out_0, out_1):
             qw(1)
             pp(0, 1, "g")
             pp(1, 1, "g")
-            rl(1, 0, 1, "s")
-            rl(1, 1, 2, "s")
-            rl(1, 2, 3, "s")
-            rl(1, 3, 4, "s")
-            rl(1, 4, 5, "s")
-            rl(1, 5, 6, "s")
+            rl(1, 0, 2, "s")
+            rl(1, 2, 4, "s")
+            rl(1, 4, 6, "s")
             av(1, 0)
             sx(1, 0)
             mm(0, 1)
@@ -397,7 +396,7 @@ def tile_tubeletembedding_kernel(tc, video, W, b, pos_embed, out_0, out_1):
             rc(0)
             pp(2, 0, "v")
             sx(1, 1)
-            fm(0, "s")
+            fm(0, "g")
             ev(2, 1)
             ga(2, 1)
             ev(3, 1)

@@ -479,6 +479,5 @@ def tile_tubeletembedding_kernel(tc, video, W, b, pos_embed, out_0, out_1):
             rd(8)
             rc(8)
             fm(8, "v")
-            ct(8, "s", 0, 384)
-            ct(8, "v", 384, 1024)
+            ct(8, "v", 0, 1024)
             s8(8)

@@ -405,63 +405,63 @@ def tile_tubeletembedding_kernel(tc, video, W, b, pos_embed, out_0, out_1):
             s8(0)
             mm(4, 0)
             mm(4, 1)
+            mm(5, 0)
+            mm(5, 1)
             rd(1)
             av(4, 0)
             sx(4, 0)
             rc(1)
             sx(2, 1)
-            fm(1, "s")
             ev(4, 1)
             ga(4, 1)
             pp(2, 1, "g")
+            fm(1, "s")
+            ev(5, 1)
+            ga(5, 1)
             ct(1, "s", 0, 1024)
             s8(1)
-            mm(5, 0)
-            mm(5, 1)
+            mm(6, 0)
+            mm(6, 1)
             rd(2)
             av(5, 0)
             sx(5, 0)
             rc(2)
             sx(3, 1)
             fm(2, "s")
-            ev(5, 1)
-            ga(5, 1)
+            ev(6, 1)
+            ga(6, 1)
             ct(2, "s", 0, 1024)
             s8(2)
-            mm(6, 0)
-            mm(6, 1)
+            mm(7, 0)
+            mm(7, 1)
             rd(3)
             av(6, 0)
             sx(6, 0)
             rc(3)
             sx(4, 1)
             fm(3, "s")
-            ev(6, 1)
-            ga(6, 1)
+            ev(7, 1)
+            ga(7, 1)
             ct(3, "s", 0, 1024)
             s8(3)
-            mm(7, 0)
-            mm(7, 1)
+            mm(8, 0)
+            mm(8, 1)
             rd(4)
             av(7, 0)
             sx(7, 0)
             rc(4)
             sx(5, 1)
             fm(4, "s")
-            ev(7, 1)
-            ga(7, 1)
+            ev(8, 1)
+            ga(8, 1)
             ct(4, "s", 0, 1024)
             s8(4)
-            mm(8, 0)
-            mm(8, 1)
             rd(5)
             av(8, 0)
             sx(8, 0)
             rc(5)
             sx(6, 1)
             fm(5, "s")
-            ev(8, 1)
-            ga(8, 1)
             ct(5, "s", 0, 1024)
             s8(5)
             rd(6)

@@ -61,6 +61,7 @@ def tile_tubeletembedding_kernel(tc, video, W, b, pos_embed, out_0, out_1):
         amax = keep.tile([P, 16], F32, name="amax")
         rcp = keep.tile([P, 16], F32, name="rcp")
         fac = keep.tile([P, 16], F32, name="fac")
+        gscr = keep.tile([P, 2], U8, name="gscr")
         w_view = W.rearrange("(t p) k -> p t k", p=P)
         w_words = wraw[:].bitcast(F32).rearrange("p (t w u) -> p t u w", t=8, w=128, u=2)
         banks = {}
@@ -248,6 +249,15 @@ def tile_tubeletembedding_kernel(tc, video, W, b, pos_embed, out_0, out_1):
             nc.vector.tensor_tensor(out=x_of(i)[:, sl], in0=banks[("a", i, n)][:],
                                     in1=posb[TILES[i][1]][:, sl], op=ALU.add)
 
+        def avh(i, n, q):
+            sl = slice(n * HALF + q * 256, n * HALF + (q + 1) * 256)
+            nc.vector.tensor_tensor(out=x_of(i)[:, sl], in0=banks[("a", i, n)][:, q * 256:(q + 1) * 256],
+                                    in1=posb[TILES[i][1]][:, sl], op=ALU.add)
+
+        def gate(k):
+            src = ws[:, HALF:HALF + 1] if k == 0 else vs[:, 1024:1025]
+            nc.gpsimd.tensor_copy(out=gscr[:, k:k + 1], in_=src)
+
         def ev(i, n):
             y_t = xs.tile([P, HALF], F32, name="y")
             yts[(i, n)] = y_t
@@ -314,14 +324,14 @@ def tile_tubeletembedding_kernel(tc, video, W, b, pos_embed, out_0, out_1):
         ld_v2("SP", 0, 0)
         ld_b("SP")
         ld_v2("SP", 0, 1)
-        ld_w("SP", 1)
-        warm()
         ld_p("SP", 0)
+        warm()
         ld_p("SP", 1)
+        ld_w("SP", 1)
+        ld_p("SP", 2)
         ld_v2("SP", 1, 0)
         ld_v2("SP", 1, 1)
         ms_rel(1, "v")
-        ld_p("SP", 2)
         with tc.manual_schedule():
             dm(0)
             dm(1)
@@ -335,10 +345,12 @@ def tile_tubeletembedding_kernel(tc, video, W, b, pos_embed, out_0, out_1):
             dm(6)
             cw(0, "s")
             cw(1, "s")
+            bbc(1)
             rl(0, 0, 2, "v")
             rl(0, 2, 4, "v")
-            rl(0, 4, 6, "s")
+            rl(0, 4, 6, "v")
             qw(0)
+            pp(0, 1, "g")
             tv(0, 0)
             tv(0, 1)
             dm(7)
@@ -353,18 +365,18 @@ def tile_tubeletembedding_kernel(tc, video, W, b, pos_embed, out_0, out_1):
             pp(1, 0, "v")
             qv(0)
             qv(1)
+            pp(2, 0, "v")
             mm(0, 0)
             mm(1, 0)
             mm(2, 0)
             mm(3, 0)
             cw(2, "s")
             cw(3, "s")
-            bbc(1)
+            qw(1)
+            gate(0)
+            pp(1, 1, "g")
             av(0, 0)
             sx(0, 0)
-            qw(1)
-            pp(0, 1, "g")
-            pp(1, 1, "g")
             rl(1, 0, 2, "s")
             rl(1, 2, 4, "s")
             rl(1, 4, 6, "s")
@@ -372,19 +384,19 @@ def tile_tubeletembedding_kernel(tc, video, W, b, pos_embed, out_0, out_1):
             sx(1, 0)
             mm(0, 1)
             mm(1, 1)
-            mm(2, 1)
-            mm(3, 1)
             tv(1, 0)
             tv(1, 1)
             tv(1, 2)
+            mm(2, 1)
+            mm(3, 1)
             ev(1, 1)
             ga(1, 1)
             av(2, 0)
             sx(2, 0)
-            av(3, 0)
-            sx(3, 0)
             av(0, 1)
             sx(0, 1)
+            av(3, 0)
+            sx(3, 0)
             cv(1, 0, "s")
             cv(1, 1, "s")
             cv(1, 2, "s")
@@ -394,7 +406,6 @@ def tile_tubeletembedding_kernel(tc, video, W, b, pos_embed, out_0, out_1):
             qv(3)
             r2q()
             rc(0)
-            pp(2, 0, "v")
             sx(1, 1)
             fm(0, "g")
             ev(2, 1)

@@ -351,6 +351,8 @@ def tile_tubeletembedding_kernel(tc, video, W, b, pos_embed, out_0, out_1):
             rl(0, 4, 6, "v")
             qw(0)
             pp(0, 1, "g")
+            pp(1, 1, "g")
+            pp(2, 1, "g")
             tv(0, 0)
             tv(0, 1)
             dm(7)
@@ -373,8 +375,6 @@ def tile_tubeletembedding_kernel(tc, video, W, b, pos_embed, out_0, out_1):
             cw(2, "s")
             cw(3, "s")
             qw(1)
-            gate(0)
-            pp(1, 1, "g")
             av(0, 0)
             sx(0, 0)
             rl(1, 0, 2, "s")
@@ -425,7 +425,6 @@ def tile_tubeletembedding_kernel(tc, video, W, b, pos_embed, out_0, out_1):
             sx(2, 1)
             ev(4, 1)
             ga(4, 1)
-            pp(2, 1, "g")
             fm(1, "s")
             ev(5, 1)
             ga(5, 1)

@@ -5,7 +5,6 @@ from concourse.masks import make_identity
 
 F32 = mybir.dt.float32
 BF16 = mybir.dt.bfloat16
-I32 = mybir.dt.int32
 U32 = mybir.dt.uint32
 U8 = mybir.dt.uint8
 FP8X4 = mybir.dt.float8_e4m3fn_x4
@@ -19,6 +18,10 @@ FLOPS = 2 * 1152 * 512 * 1024
 P = 128
 EMBED = 1024
 HALF = 512
+ROWS = 96
+FRAME = 1536
+N_TILES = 9
+LAST = N_TILES - 1
 TILES = [(0, 0), (1, 0), (0, 1), (1, 1), (2, 0), (3, 0), (2, 1), (3, 1), (4, 2)]
 
 
@@ -26,7 +29,7 @@ def tile_tubeletembedding_kernel(tc, video, W, b, pos_embed, out_0, out_1):
     nc = tc.nc
     with ExitStack() as ctx:
         keep = ctx.enter_context(tc.tile_pool(name="keep", bufs=1))
-        xs = ctx.enter_context(tc.tile_pool(name="xs", bufs=9))
+        xs = ctx.enter_context(tc.tile_pool(name="xs", bufs=N_TILES))
         psum = ctx.enter_context(tc.psum_pool(name="psum", bufs=8))
 
         brow = keep.tile([P, EMBED], BF16, name="brow")
@@ -39,8 +42,8 @@ def tile_tubeletembedding_kernel(tc, video, W, b, pos_embed, out_0, out_1):
         raws = []
         relaid = []
         for bp in range(2):
-            raw_t = keep.tile([P, 3072], BF16, name="raw%d" % bp)
-            rel_t = keep.tile([P, 1536], F32, name="rel%d" % bp)
+            raw_t = keep.tile([P, 2 * FRAME], BF16, name="raw%d" % bp)
+            rel_t = keep.tile([P, FRAME], F32, name="rel%d" % bp)
             raws.append(raw_t)
             relaid.append(rel_t)
         pos_sb = []
@@ -61,92 +64,45 @@ def tile_tubeletembedding_kernel(tc, video, W, b, pos_embed, out_0, out_1):
         amax = keep.tile([P, 16], F32, name="amax")
         rcp = keep.tile([P, 16], F32, name="rcp")
         fac = keep.tile([P, 16], F32, name="fac")
-        gscr = keep.tile([P, 2], U8, name="gscr")
-        w_view = W.rearrange("(t p) k -> p t k", p=P)
         w_words = wraw[:].bitcast(F32).rearrange("p (t w u) -> p t u w", t=8, w=128, u=2)
         banks = {}
-        xts = {}
-        yts = {}
-        o8s = {}
-        queues = {"SP": nc.sync, "S": nc.scalar, "G": nc.gpsimd}
-
-        def copy_on(eng, out, in_):
-            if eng == "v":
-                nc.vector.tensor_copy(out=out, in_=in_)
-            elif eng == "g":
-                nc.gpsimd.tensor_copy(out=out, in_=in_)
-            else:
-                nc.scalar.copy(out=out, in_=in_)
+        x_tiles = {}
+        y_tiles = {}
+        byte_tiles = {}
 
         def new_bank(key):
             bank = psum.tile([P, HALF], F32, name="bank")
             banks[key] = bank
             return bank
 
-        def ms_brow(e):
-            if e == "v":
-                nc.vector.memset(brow[:].bitcast(I32), 0)
-            else:
-                nc.gpsimd.memset(brow[:].bitcast(F32), 0.0)
 
-        def ms_zero(e):
-            if e == "v":
-                nc.vector.memset(zeros[:], 0.0)
-            else:
-                nc.gpsimd.memset(zeros[:], 0.0)
-
-        def ms_dmy():
-            nc.gpsimd.memset(dmy[:], 0.0)
-
-        def ms_rel(bp, e):
-            if e == "v":
-                nc.vector.memset(relaid[bp][96:128, :], 0.0)
-            else:
-                nc.gpsimd.memset(relaid[bp][96:128, :], 0.0)
-
-        def ident():
-            make_identity(nc, idn[:])
-
-        def ones(e):
-            if e == "v":
-                nc.vector.memset(one[:], 1.0)
-            else:
-                nc.gpsimd.memset(one[:], 1.0)
-
-        def warm():
-            nc.scalar.activation(out=wrm[:], in_=zeros[:], func=ACT.Identity)
-
-        def ld_b(q):
-            queues[q].dma_start(out=brow[0:1, :], in_=b.rearrange("(o e) -> o e", o=1))
-
-        def ld_w(q, h):
-            queues[q].dma_start(
+        def load_w(h):
+            nc.sync.dma_start(
                 out=wraw[:, h * 2048:(h + 1) * 2048],
                 in_=W[h * 512:(h + 1) * 512, :].rearrange("(p t) k -> p (t k)", t=4))
 
-        def ld_wq(q, tp):
-            queues[q].dma_start(
-                out=wraw[:, tp * 1024:(tp + 1) * 1024].rearrange("p (t k) -> p t k", t=2),
-                in_=w_view[:, 2 * tp:2 * tp + 2, :])
-
-        def ld_v2(q, bp, ts):
+        def load_video(bp, ts):
             src = video[2 * bp:2 * bp + 2, :, 0].rearrange(
                 "b (d t) (i y) x -> t (b d) i (y x)", t=2, y=16)
-            queues[q].dma_start(out=raws[bp][0:96, ts * 1536:(ts + 1) * 1536], in_=src[ts])
+            nc.sync.dma_start(out=raws[bp][0:ROWS, ts * FRAME:(ts + 1) * FRAME], in_=src[ts])
 
-        def ld_p(q, t):
-            if t < 2:
-                queues[q].dma_start(out=pos_sb[t][:], in_=pos_embed[0, t * P:(t + 1) * P, :])
+        def load_b():
+            nc.sync.dma_start(out=brow[0:1, :], in_=b.rearrange("(o e) -> o e", o=1))
+
+        def load_pos(h):
+            if h < 2:
+                nc.sync.dma_start(out=pos_sb[h][:], in_=pos_embed[0, h * P:(h + 1) * P, :])
             else:
-                for bb in range(4):
-                    queues[q].dma_start(out=pos_sb[2][bb:128:4, :], in_=pos_embed[0, 256:288, :])
+                for e in range(4):
+                    nc.sync.dma_start(out=pos_sb[2][e:128:4, :], in_=pos_embed[0, 256:288, :])
 
-        def dm(k):
+
+        def keep_pe_busy():
             if "dm" not in banks:
                 new_bank("dm")
             nc.tensor.matmul(out=banks["dm"][:, 0:P], lhsT=dmy[:], rhs=dmy[:], start=True, stop=True)
 
-        def tw(tp):
+        def transpose_w(tp):
             bank = new_bank(("w", tp))
             for t in range(2):
                 for u in range(2):
@@ -154,89 +110,22 @@ def tile_tubeletembedding_kernel(tc, video, W, b, pos_embed, out_0, out_1):
                     nc.tensor.transpose(out=bank[:, s * P:(s + 1) * P],
                                         in_=w_words[:, 2 * tp + t, u, :], identity=idn[:])
 
-        def cw(tp, e):
-            h, a = divmod(tp, 2)
-            copy_on(e, gw[:, h * 1024:(h + 1) * 1024].rearrange("p (e a s) -> p a e s", a=2, s=4)[:, a],
-                    banks[("w", tp)][:].rearrange("p (s e) -> p e s", s=4))
-
-        def qw(h):
-            nc.vector.quantize_mx(out=wc[:, h * HALF:(h + 1) * HALF].bitcast(FP8X4),
-                                  scales=ws[:, h * HALF:(h + 1) * HALF],
-                                  in_=gw[:, h * 1024:(h + 1) * 1024].bitcast(BF16))
-
-        def qwq(tp):
-            nc.vector.quantize_mx(out=wc[:, tp * 256:(tp + 1) * 256].bitcast(FP8X4),
-                                  scales=ws[:, tp * 256:(tp + 1) * 256],
-                                  in_=gw[:, tp * 512:(tp + 1) * 512].bitcast(BF16))
-
-        def rl(bp, j0, j1, e):
-            src = raws[bp][0:96, :].bitcast(F32).rearrange(
-                "p (r j q u) -> p j u r q", r=32, j=6, q=4, u=2)
-            dst = relaid[bp][0:96, :].rearrange("p (j u r q) -> p j u r q", j=6, u=2, r=32, q=4)
-            if j1 - j0 == 1:
-                copy_on(e, dst[:, j0], src[:, j0])
-            else:
-                copy_on(e, dst[:, j0:j1], src[:, j0:j1])
-
-        def tv(bp, jp):
+        def transpose_video(bp, jp):
             bank = new_bank(("v", bp, jp))
             for s in range(4):
                 c = 4 * jp + s
                 nc.tensor.transpose(out=bank[:, s * P:(s + 1) * P],
                                     in_=relaid[bp][:, c * P:(c + 1) * P], identity=idn[:])
 
-        def cv(bp, jp, e):
-            dst = gv[:, bp * 1152:(bp + 1) * 1152].rearrange(
-                "p (c w) -> p c w", w=12)[:, :, 4 * jp:4 * jp + 4]
-            src = banks[("v", bp, jp)][:].rearrange("p (s c) -> p c s", s=4)[:, 0:96, :]
-            copy_on(e, dst, src)
-
-        def qv(bb):
-            nc.vector.quantize_mx(out=vc[:, bb * 256:(bb + 1) * 256].bitcast(FP8X4),
-                                  scales=vs[:, bb * 256:(bb + 1) * 256],
-                                  in_=gv[:, bb * 576:bb * 576 + 512].bitcast(BF16))
-
-        def r2c(e):
-            copy_on(
-                e,
-                g2[:].rearrange("p (n b w) -> p n b w", b=4, w=2),
-                gv[:].rearrange("p (b x) -> p b x", b=4)[:, :, 512:576].rearrange(
-                    "p b (n w) -> p n b w", w=2))
-
-        def r2q():
-            nc.vector.quantize_mx(out=vc[:, 1024:1152].bitcast(FP8X4), scales=vs[:, 1024:1152],
-                                  in_=g2[:].bitcast(BF16))
-
-        def pb():
+        def spread_b():
             for h in range(2):
                 bank = new_bank(("b", h))
                 nc.tensor.matmul(out=bank[:], lhsT=one[:], rhs=brow[:, h * HALF:(h + 1) * HALF],
                                  start=True, stop=True)
 
-        def bbc(h):
-            nc.scalar.copy(out=bbt[:, h * HALF:(h + 1) * HALF], in_=banks[("b", h)][:])
-
-        def pp(t, h, e):
-            sl = slice(h * HALF, (h + 1) * HALF)
-            if e == "v":
-                nc.vector.tensor_tensor(out=posb[t][:, sl], in0=banks[("b", h)][:], in1=pos_sb[t][:, sl],
-                                        op=ALU.add)
-            else:
-                nc.gpsimd.tensor_tensor(out=posb[t][:, sl], in0=pos_sb[t][:, sl], in1=bbt[:, sl],
-                                        op=ALU.add)
-
-        def ppw(t):
-            nc.gpsimd.tensor_tensor(out=posb[t][:], in0=pos_sb[t][:], in1=bbt[:], op=ALU.add)
-
-        def x_of(i):
-            if i not in xts:
-                x_t = xs.tile([P, EMBED], F32, name="x")
-                xts[i] = x_t
-            return xts[i]
-
-        def mm(i, n):
-            bb, h = TILES[i]
-            c0 = 1024 if h == 2 else (2 * bb + h) * P
+        def mx_pass(i, n):
+            e, h = TILES[i]
+            c0 = 1024 if h == 2 else (2 * e + h) * P
             acc = new_bank(("a", i, n))
             nc.tensor.matmul_mx(out=acc[:],
                                 lhsT=vc[:, c0:c0 + P].bitcast(FP8X4), lhsT_scale=vs[:, c0:c0 + P],
@@ -244,250 +133,246 @@ def tile_tubeletembedding_kernel(tc, video, W, b, pos_embed, out_0, out_1):
                                 rhs_scale=ws[:, n * HALF:(n + 1) * HALF],
                                 start=True, stop=True)
 
-        def av(i, n):
+
+        def reorder_views(bp, jp):
+            src = raws[bp][0:ROWS, :].bitcast(F32).rearrange(
+                "p (r j q u) -> p j u r q", r=32, j=6, q=4, u=2)
+            dst = relaid[bp][0:ROWS, :].rearrange("p (j u r q) -> p j u r q", j=6, u=2, r=32, q=4)
+            return dst[:, 2 * jp:2 * jp + 2], src[:, 2 * jp:2 * jp + 2]
+
+        def reorder_on_vector(bp, jp):
+            dst, src = reorder_views(bp, jp)
+            nc.vector.tensor_copy(out=dst, in_=src)
+
+        def reorder_on_scalar(bp, jp):
+            dst, src = reorder_views(bp, jp)
+            nc.scalar.copy(out=dst, in_=src)
+
+
+        def copy_w(tp):
+            h, a = divmod(tp, 2)
+            nc.scalar.copy(
+                out=gw[:, h * 1024:(h + 1) * 1024].rearrange("p (e a s) -> p a e s", a=2, s=4)[:, a],
+                in_=banks[("w", tp)][:].rearrange("p (s e) -> p e s", s=4))
+
+        def copy_video(bp, jp):
+            dst = gv[:, bp * 1152:(bp + 1) * 1152].rearrange(
+                "p (c w) -> p c w", w=12)[:, :, 4 * jp:4 * jp + 4]
+            src = banks[("v", bp, jp)][:].rearrange("p (s c) -> p c s", s=4)[:, 0:ROWS, :]
+            nc.scalar.copy(out=dst, in_=src)
+
+        def gather_last_tile():
+            nc.scalar.copy(
+                out=g2[:].rearrange("p (n b w) -> p n b w", b=4, w=2),
+                in_=gv[:].rearrange("p (b x) -> p b x", b=4)[:, :, 512:576].rearrange(
+                    "p b (n w) -> p n b w", w=2))
+
+        def copy_b_for_gpsimd():
+            nc.scalar.copy(out=bbt[:, HALF:EMBED], in_=banks[("b", 1)][:])
+
+        def copy_second_bank(i):
+            y_t = xs.tile([P, HALF], F32, name="y")
+            y_tiles[i] = y_t
+            nc.scalar.copy(out=y_t[:], in_=banks[("a", i, 1)][:])
+
+        def factor_on_scalar(i):
+            nc.scalar.activation(out=fac[:, i:i + 1], in_=rcp[:, i:i + 1], func=ACT.Identity, scale=448.0)
+
+        def new_byte_tile(i):
+            o_t = xs.tile([P, EMBED], FP8, name="o8")
+            byte_tiles[i] = o_t
+            return o_t
+
+        def cast_on_scalar(i):
+            nc.scalar.activation(out=new_byte_tile(i)[:, 0:EMBED], in_=x_tiles[i][:, 0:EMBED], func=ACT.Identity,
+                                 scale=fac[:, i:i + 1], bias=zeros[:, 0:1], saturate=False)
+
+
+        def quantize_w(h):
+            nc.vector.quantize_mx(out=wc[:, h * HALF:(h + 1) * HALF].bitcast(FP8X4),
+                                  scales=ws[:, h * HALF:(h + 1) * HALF],
+                                  in_=gw[:, h * 1024:(h + 1) * 1024].bitcast(BF16))
+
+        def quantize_video(e):
+            nc.vector.quantize_mx(out=vc[:, e * 256:(e + 1) * 256].bitcast(FP8X4),
+                                  scales=vs[:, e * 256:(e + 1) * 256],
+                                  in_=gv[:, e * 576:e * 576 + 512].bitcast(BF16))
+
+        def quantize_last_tile():
+            nc.vector.quantize_mx(out=vc[:, 1024:1152].bitcast(FP8X4), scales=vs[:, 1024:1152],
+                                  in_=g2[:].bitcast(BF16))
+
+        def pos_plus_b_on_vector(h):
+            nc.vector.tensor_tensor(out=posb[h][:, 0:HALF], in0=banks[("b", 0)][:], in1=pos_sb[h][:, 0:HALF],
+                                    op=ALU.add)
+
+        def x_of(i):
+            if i not in x_tiles:
+                x_t = xs.tile([P, EMBED], F32, name="x")
+                x_tiles[i] = x_t
+            return x_tiles[i]
+
+        def add_on_vector(i, n):
             sl = slice(n * HALF, (n + 1) * HALF)
             nc.vector.tensor_tensor(out=x_of(i)[:, sl], in0=banks[("a", i, n)][:],
                                     in1=posb[TILES[i][1]][:, sl], op=ALU.add)
 
-        def avh(i, n, q):
-            sl = slice(n * HALF + q * 256, n * HALF + (q + 1) * 256)
-            nc.vector.tensor_tensor(out=x_of(i)[:, sl], in0=banks[("a", i, n)][:, q * 256:(q + 1) * 256],
-                                    in1=posb[TILES[i][1]][:, sl], op=ALU.add)
-
-        def gate(k):
-            src = ws[:, HALF:HALF + 1] if k == 0 else vs[:, 1024:1025]
-            nc.gpsimd.tensor_copy(out=gscr[:, k:k + 1], in_=src)
-
-        def ev(i, n):
-            y_t = xs.tile([P, HALF], F32, name="y")
-            yts[(i, n)] = y_t
-            nc.scalar.copy(out=y_t[:], in_=banks[("a", i, n)][:])
-
-        def ga(i, n):
-            sl = slice(n * HALF, (n + 1) * HALF)
-            nc.gpsimd.tensor_tensor(out=x_of(i)[:, sl], in0=yts[(i, n)][:],
-                                    in1=posb[TILES[i][1]][:, sl], op=ALU.add)
-
-        def sx(i, n):
-            bb, h = TILES[i]
-            sl = slice(n * HALF, (n + 1) * HALF)
-            if h == 2:
-                nc.sync.dma_start(out=out_0[:, 256:288, sl].rearrange("b n e -> n b e"), in_=xts[i][:, sl])
-            else:
-                nc.sync.dma_start(out=out_0[bb, h * P:(h + 1) * P, sl], in_=xts[i][:, sl])
-
-        def rd(i):
-            nc.vector.tensor_reduce(out=amax[:, i:i + 1], in_=xts[i][:], axis=AX.X, op=ALU.max,
+        def row_max(i):
+            nc.vector.tensor_reduce(out=amax[:, i:i + 1], in_=x_tiles[i][:], axis=AX.X, op=ALU.max,
                                     apply_absolute_value=True)
 
-        def rc(i):
+        def reciprocal(i):
             nc.vector.reciprocal(out=rcp[:, i:i + 1], in_=amax[:, i:i + 1])
 
-        def fm(i, e):
-            if e == "g":
-                nc.gpsimd.tensor_scalar(out=fac[:, i:i + 1], in0=rcp[:, i:i + 1], scalar1=448.0,
-                                        scalar2=None, op0=ALU.mult)
-            elif e == "v":
-                nc.vector.tensor_scalar(out=fac[:, i:i + 1], in0=rcp[:, i:i + 1], scalar1=448.0,
-                                        scalar2=None, op0=ALU.mult)
-            else:
-                nc.scalar.activation(out=fac[:, i:i + 1], in_=rcp[:, i:i + 1], func=ACT.Identity,
-                                     scale=448.0)
+        def factor_on_vector(i):
+            nc.vector.tensor_scalar(out=fac[:, i:i + 1], in0=rcp[:, i:i + 1], scalar1=448.0,
+                                    scalar2=None, op0=ALU.mult)
 
-        def ct(i, e, lo, hi):
-            if i not in o8s:
-                o_t = xs.tile([P, EMBED], FP8, name="o8")
-                o8s[i] = o_t
-            if e == "v":
-                nc.vector.tensor_scalar(out=o8s[i][:, lo:hi], in0=xts[i][:, lo:hi],
-                                        scalar1=fac[:, i:i + 1], scalar2=None, op0=ALU.mult,
-                                        saturate=False)
-            else:
-                nc.scalar.activation(out=o8s[i][:, lo:hi], in_=xts[i][:, lo:hi], func=ACT.Identity,
-                                     scale=fac[:, i:i + 1], bias=zeros[:, 0:1], saturate=False)
+        def cast_on_vector(i):
+            nc.vector.tensor_scalar(out=new_byte_tile(i)[:, 0:EMBED], in0=x_tiles[i][:, 0:EMBED],
+                                    scalar1=fac[:, i:i + 1], scalar2=None, op0=ALU.mult,
+                                    saturate=False)
 
-        def s8(i):
-            bb, h = TILES[i]
+
+        def pos_plus_b_on_gpsimd(h):
+            nc.gpsimd.tensor_tensor(out=posb[h][:, HALF:EMBED], in0=pos_sb[h][:, HALF:EMBED],
+                                    in1=bbt[:, HALF:EMBED], op=ALU.add)
+
+        def add_on_gpsimd(i):
+            nc.gpsimd.tensor_tensor(out=x_of(i)[:, HALF:EMBED], in0=y_tiles[i][:],
+                                    in1=posb[TILES[i][1]][:, HALF:EMBED], op=ALU.add)
+
+
+        def store_x(i, n):
+            e, h = TILES[i]
+            sl = slice(n * HALF, (n + 1) * HALF)
+            if h == 2:
+                nc.sync.dma_start(out=out_0[:, 256:288, sl].rearrange("b n e -> n b e"), in_=x_tiles[i][:, sl])
+            else:
+                nc.sync.dma_start(out=out_0[e, h * P:(h + 1) * P, sl], in_=x_tiles[i][:, sl])
+
+        def store_bytes(i):
+            e, h = TILES[i]
             if h == 2:
                 dst = out_1[:, 256:288, :].rearrange("b n e -> n b e")
             else:
-                dst = out_1[bb, h * P:(h + 1) * P, :]
-            nc.sync.dma_start(out=dst, in_=o8s[i][:].bitcast(U8))
+                dst = out_1[e, h * P:(h + 1) * P, :]
+            nc.sync.dma_start(out=dst, in_=byte_tiles[i][:].bitcast(U8))
 
-        ms_brow("g")
-        ms_dmy()
-        ms_zero("v")
-        ms_rel(0, "v")
-        ident()
-        ones("g")
-        ld_w("SP", 0)
-        ld_v2("SP", 0, 0)
-        ld_b("SP")
-        ld_v2("SP", 0, 1)
-        ld_p("SP", 0)
-        warm()
-        ld_p("SP", 1)
-        ld_w("SP", 1)
-        ld_p("SP", 2)
-        ld_v2("SP", 1, 0)
-        ld_v2("SP", 1, 1)
-        ms_rel(1, "v")
+        nc.gpsimd.memset(brow[:].bitcast(F32), 0.0)
+        nc.gpsimd.memset(dmy[:], 0.0)
+        nc.vector.memset(zeros[:], 0.0)
+        nc.vector.memset(relaid[0][ROWS:P, :], 0.0)
+        make_identity(nc, idn[:])
+        nc.gpsimd.memset(one[:], 1.0)
+        load_w(0)
+        load_video(0, 0)
+        load_b()
+        load_video(0, 1)
+        load_pos(0)
+        nc.scalar.activation(out=wrm[:], in_=zeros[:], func=ACT.Identity)
+        load_pos(1)
+        load_w(1)
+        load_pos(2)
+        load_video(1, 0)
+        load_video(1, 1)
+        nc.vector.memset(relaid[1][ROWS:P, :], 0.0)
+
         with tc.manual_schedule():
-            dm(0)
-            dm(1)
-            dm(2)
-            dm(3)
-            dm(4)
-            tw(0)
-            tw(1)
-            dm(5)
-            pb()
-            dm(6)
-            cw(0, "s")
-            cw(1, "s")
-            bbc(1)
-            rl(0, 0, 2, "v")
-            rl(0, 2, 4, "v")
-            rl(0, 4, 6, "v")
-            qw(0)
-            pp(0, 1, "g")
-            pp(1, 1, "g")
-            pp(2, 1, "g")
-            tv(0, 0)
-            tv(0, 1)
-            dm(7)
-            tv(0, 2)
-            tw(2)
-            dm(8)
-            tw(3)
-            cv(0, 0, "s")
-            cv(0, 1, "s")
-            cv(0, 2, "s")
-            pp(0, 0, "v")
-            pp(1, 0, "v")
-            qv(0)
-            qv(1)
-            pp(2, 0, "v")
-            mm(0, 0)
-            mm(1, 0)
-            mm(2, 0)
-            mm(3, 0)
-            cw(2, "s")
-            cw(3, "s")
-            qw(1)
-            av(0, 0)
-            sx(0, 0)
-            rl(1, 0, 2, "s")
-            rl(1, 2, 4, "s")
-            rl(1, 4, 6, "s")
-            av(1, 0)
-            sx(1, 0)
-            mm(0, 1)
-            mm(1, 1)
-            tv(1, 0)
-            tv(1, 1)
-            tv(1, 2)
-            mm(2, 1)
-            mm(3, 1)
-            ev(1, 1)
-            ga(1, 1)
-            av(2, 0)
-            sx(2, 0)
-            av(0, 1)
-            sx(0, 1)
-            av(3, 0)
-            sx(3, 0)
-            cv(1, 0, "s")
-            cv(1, 1, "s")
-            cv(1, 2, "s")
-            r2c("s")
-            rd(0)
-            qv(2)
-            qv(3)
-            r2q()
-            rc(0)
-            sx(1, 1)
-            fm(0, "g")
-            ev(2, 1)
-            ga(2, 1)
-            ev(3, 1)
-            ga(3, 1)
-            ct(0, "s", 0, 1024)
-            s8(0)
-            mm(4, 0)
-            mm(4, 1)
-            mm(5, 0)
-            mm(5, 1)
-            rd(1)
-            av(4, 0)
-            sx(4, 0)
-            rc(1)
-            sx(2, 1)
-            ev(4, 1)
-            ga(4, 1)
-            fm(1, "s")
-            ev(5, 1)
-            ga(5, 1)
-            ct(1, "s", 0, 1024)
-            s8(1)
-            mm(6, 0)
-            mm(6, 1)
-            rd(2)
-            av(5, 0)
-            sx(5, 0)
-            rc(2)
-            sx(3, 1)
-            fm(2, "s")
-            ev(6, 1)
-            ga(6, 1)
-            ct(2, "s", 0, 1024)
-            s8(2)
-            mm(7, 0)
-            mm(7, 1)
-            rd(3)
-            av(6, 0)
-            sx(6, 0)
-            rc(3)
-            sx(4, 1)
-            fm(3, "s")
-            ev(7, 1)
-            ga(7, 1)
-            ct(3, "s", 0, 1024)
-            s8(3)
-            mm(8, 0)
-            mm(8, 1)
-            rd(4)
-            av(7, 0)
-            sx(7, 0)
-            rc(4)
-            sx(5, 1)
-            fm(4, "s")
-            ev(8, 1)
-            ga(8, 1)
-            ct(4, "s", 0, 1024)
-            s8(4)
-            rd(5)
-            av(8, 0)
-            sx(8, 0)
-            rc(5)
-            sx(6, 1)
-            fm(5, "s")
-            ct(5, "s", 0, 1024)
-            s8(5)
-            rd(6)
-            rc(6)
-            sx(7, 1)
-            fm(6, "s")
-            ct(6, "s", 0, 1024)
-            s8(6)
-            rd(7)
-            rc(7)
-            sx(8, 1)
-            fm(7, "s")
-            ct(7, "s", 0, 1024)
-            s8(7)
-            rd(8)
-            rc(8)
-            fm(8, "v")
-            ct(8, "v", 0, 1024)
-            s8(8)
+            for k in range(5):
+                keep_pe_busy()
+            transpose_w(0)
+            transpose_w(1)
+            keep_pe_busy()
+            spread_b()
+            keep_pe_busy()
+            copy_w(0)
+            copy_w(1)
+            copy_b_for_gpsimd()
+            for jp in range(3):
+                reorder_on_vector(0, jp)
+            quantize_w(0)
+            for h in range(3):
+                pos_plus_b_on_gpsimd(h)
+            transpose_video(0, 0)
+            transpose_video(0, 1)
+            keep_pe_busy()
+            transpose_video(0, 2)
+            transpose_w(2)
+            keep_pe_busy()
+            transpose_w(3)
+            for jp in range(3):
+                copy_video(0, jp)
+            pos_plus_b_on_vector(0)
+            pos_plus_b_on_vector(1)
+            quantize_video(0)
+            quantize_video(1)
+            pos_plus_b_on_vector(2)
+            for i in range(4):
+                mx_pass(i, 0)
+            copy_w(2)
+            copy_w(3)
+            quantize_w(1)
+            add_on_vector(0, 0)
+            store_x(0, 0)
+            for jp in range(3):
+                reorder_on_scalar(1, jp)
+            add_on_vector(1, 0)
+            store_x(1, 0)
+            mx_pass(0, 1)
+            mx_pass(1, 1)
+            for jp in range(3):
+                transpose_video(1, jp)
+            mx_pass(2, 1)
+            mx_pass(3, 1)
+            copy_second_bank(1)
+            add_on_gpsimd(1)
+            add_on_vector(2, 0)
+            store_x(2, 0)
+            add_on_vector(0, 1)
+            store_x(0, 1)
+            add_on_vector(3, 0)
+            store_x(3, 0)
+            for jp in range(3):
+                copy_video(1, jp)
+            gather_last_tile()
+            row_max(0)
+            quantize_video(2)
+            quantize_video(3)
+            quantize_last_tile()
+            reciprocal(0)
+            store_x(1, 1)
+            for i in (2, 3):
+                copy_second_bank(i)
+                add_on_gpsimd(i)
+            factor_on_scalar(0)
+            cast_on_scalar(0)
+            store_bytes(0)
+            mx_pass(4, 0)
+            mx_pass(4, 1)
+            copy_second_ahead = 4
+            add_first_ahead = 3
+            for i in range(1, LAST):
+                if i + copy_second_ahead <= LAST:
+                    mx_pass(i + copy_second_ahead, 0)
+                    mx_pass(i + copy_second_ahead, 1)
+                row_max(i)
+                if i + add_first_ahead <= LAST:
+                    add_on_vector(i + add_first_ahead, 0)
+                    store_x(i + add_first_ahead, 0)
+                reciprocal(i)
+                store_x(i + 1, 1)
+                if i == 1:
+                    copy_second_bank(4)
+                    add_on_gpsimd(4)
+                factor_on_scalar(i)
+                if i + copy_second_ahead <= LAST:
+                    copy_second_bank(i + copy_second_ahead)
+                    add_on_gpsimd(i + copy_second_ahead)
+                cast_on_scalar(i)
+                store_bytes(i)
+            row_max(LAST)
+            reciprocal(LAST)
+            factor_on_vector(LAST)
+            cast_on_vector(LAST)
+            store_bytes(LAST)

from contextlib import ExitStack

import concourse.mybir as mybir
from concourse.masks import make_identity

F32 = mybir.dt.float32
BF16 = mybir.dt.bfloat16
U32 = mybir.dt.uint32
U8 = mybir.dt.uint8
FP8X4 = mybir.dt.float8_e4m3fn_x4
FP8 = mybir.dt.float8_e4m3fn
ALU = mybir.AluOpType
ACT = mybir.ActivationFunctionType
AX = mybir.AxisListType

FLOPS = 2 * 1152 * 512 * 1024

P = 128
EMBED = 1024
HALF = 512
ROWS = 96
FRAME = 1536
N_TILES = 9
LAST = N_TILES - 1
TILES = [(0, 0), (1, 0), (0, 1), (1, 1), (2, 0), (3, 0), (2, 1), (3, 1), (4, 2)]


def tile_tubeletembedding_kernel(tc, video, W, b, pos_embed, out_0, out_1):
    nc = tc.nc
    with ExitStack() as ctx:
        keep = ctx.enter_context(tc.tile_pool(name="keep", bufs=1))
        xs = ctx.enter_context(tc.tile_pool(name="xs", bufs=N_TILES))
        psum = ctx.enter_context(tc.psum_pool(name="psum", bufs=8))

        brow = keep.tile([P, EMBED], BF16, name="brow")
        zeros = keep.tile([P, 1], F32, name="zeros")
        idn = keep.tile([P, P], F32, name="idn")
        one = keep.tile([P, P], BF16, name="one")
        wrm = keep.tile([P, 1], F32, name="wrm")
        dmy = keep.tile([P, P], F32, name="dmy")
        wraw = keep.tile([P, 8 * 512], BF16, name="wraw")
        raws = []
        relaid = []
        for bp in range(2):
            raw_t = keep.tile([P, 2 * FRAME], BF16, name="raw%d" % bp)
            rel_t = keep.tile([P, FRAME], F32, name="rel%d" % bp)
            raws.append(raw_t)
            relaid.append(rel_t)
        pos_sb = []
        posb = []
        for h in range(3):
            pos_t = keep.tile([P, EMBED], BF16, name="pos%d" % h)
            pos_sb.append(pos_t)
            pt = keep.tile([P, EMBED], F32, name="posb%d" % h)
            posb.append(pt)
        bbt = keep.tile([P, EMBED], F32, name="bbt")
        gw = keep.tile([P, 2048], F32, name="gw", align_bytes=64)
        wc = keep.tile([P, EMBED], U32, name="wc", align_bytes=64)
        ws = keep.tile([P, EMBED], U8, name="ws", align_bytes=64)
        gv = keep.tile([P, 4 * 576], F32, name="gv", align_bytes=64)
        g2 = keep.tile([P, 256], F32, name="g2", align_bytes=64)
        vc = keep.tile([P, 1152], U32, name="vc", align_bytes=64)
        vs = keep.tile([P, 1152], U8, name="vs", align_bytes=64)
        amax = keep.tile([P, 16], F32, name="amax")
        rcp = keep.tile([P, 16], F32, name="rcp")
        fac = keep.tile([P, 16], F32, name="fac")
        w_words = wraw[:].bitcast(F32).rearrange("p (t w u) -> p t u w", t=8, w=128, u=2)
        banks = {}
        x_tiles = {}
        y_tiles = {}
        byte_tiles = {}

        def new_bank(key):
            bank = psum.tile([P, HALF], F32, name="bank")
            banks[key] = bank
            return bank


        def load_w(h):
            nc.sync.dma_start(
                out=wraw[:, h * 2048:(h + 1) * 2048],
                in_=W[h * 512:(h + 1) * 512, :].rearrange("(p t) k -> p (t k)", t=4))

        def load_video(bp, ts):
            src = video[2 * bp:2 * bp + 2, :, 0].rearrange(
                "b (d t) (i y) x -> t (b d) i (y x)", t=2, y=16)
            nc.sync.dma_start(out=raws[bp][0:ROWS, ts * FRAME:(ts + 1) * FRAME], in_=src[ts])

        def load_b():
            nc.sync.dma_start(out=brow[0:1, :], in_=b.rearrange("(o e) -> o e", o=1))

        def load_pos(h):
            if h < 2:
                nc.sync.dma_start(out=pos_sb[h][:], in_=pos_embed[0, h * P:(h + 1) * P, :])
            else:
                for e in range(4):
                    nc.sync.dma_start(out=pos_sb[2][e:128:4, :], in_=pos_embed[0, 256:288, :])


        def keep_pe_busy():
            if "dm" not in banks:
                new_bank("dm")
            nc.tensor.matmul(out=banks["dm"][:, 0:P], lhsT=dmy[:], rhs=dmy[:], start=True, stop=True)

        def transpose_w(tp):
            bank = new_bank(("w", tp))
            for t in range(2):
                for u in range(2):
                    s = 2 * t + u
                    nc.tensor.transpose(out=bank[:, s * P:(s + 1) * P],
                                        in_=w_words[:, 2 * tp + t, u, :], identity=idn[:])

        def transpose_video(bp, jp):
            bank = new_bank(("v", bp, jp))
            for s in range(4):
                c = 4 * jp + s
                nc.tensor.transpose(out=bank[:, s * P:(s + 1) * P],
                                    in_=relaid[bp][:, c * P:(c + 1) * P], identity=idn[:])

        def spread_b():
            for h in range(2):
                bank = new_bank(("b", h))
                nc.tensor.matmul(out=bank[:], lhsT=one[:], rhs=brow[:, h * HALF:(h + 1) * HALF],
                                 start=True, stop=True)

        def mx_pass(i, n):
            e, h = TILES[i]
            c0 = 1024 if h == 2 else (2 * e + h) * P
            acc = new_bank(("a", i, n))
            nc.tensor.matmul_mx(out=acc[:],
                                lhsT=vc[:, c0:c0 + P].bitcast(FP8X4), lhsT_scale=vs[:, c0:c0 + P],
                                rhs=wc[:, n * HALF:(n + 1) * HALF].bitcast(FP8X4),
                                rhs_scale=ws[:, n * HALF:(n + 1) * HALF],
                                start=True, stop=True)


        def reorder_views(bp, jp):
            src = raws[bp][0:ROWS, :].bitcast(F32).rearrange(
                "p (r j q u) -> p j u r q", r=32, j=6, q=4, u=2)
            dst = relaid[bp][0:ROWS, :].rearrange("p (j u r q) -> p j u r q", j=6, u=2, r=32, q=4)
            return dst[:, 2 * jp:2 * jp + 2], src[:, 2 * jp:2 * jp + 2]

        def reorder_on_vector(bp, jp):
            dst, src = reorder_views(bp, jp)
            nc.vector.tensor_copy(out=dst, in_=src)

        def reorder_on_scalar(bp, jp):
            dst, src = reorder_views(bp, jp)
            nc.scalar.copy(out=dst, in_=src)


        def copy_w(tp):
            h, a = divmod(tp, 2)
            nc.scalar.copy(
                out=gw[:, h * 1024:(h + 1) * 1024].rearrange("p (e a s) -> p a e s", a=2, s=4)[:, a],
                in_=banks[("w", tp)][:].rearrange("p (s e) -> p e s", s=4))

        def copy_video(bp, jp):
            dst = gv[:, bp * 1152:(bp + 1) * 1152].rearrange(
                "p (c w) -> p c w", w=12)[:, :, 4 * jp:4 * jp + 4]
            src = banks[("v", bp, jp)][:].rearrange("p (s c) -> p c s", s=4)[:, 0:ROWS, :]
            nc.scalar.copy(out=dst, in_=src)

        def gather_last_tile():
            nc.scalar.copy(
                out=g2[:].rearrange("p (n b w) -> p n b w", b=4, w=2),
                in_=gv[:].rearrange("p (b x) -> p b x", b=4)[:, :, 512:576].rearrange(
                    "p b (n w) -> p n b w", w=2))

        def copy_b_for_gpsimd():
            nc.scalar.copy(out=bbt[:, HALF:EMBED], in_=banks[("b", 1)][:])

        def copy_second_bank(i):
            y_t = xs.tile([P, HALF], F32, name="y")
            y_tiles[i] = y_t
            nc.scalar.copy(out=y_t[:], in_=banks[("a", i, 1)][:])

        def factor_on_scalar(i):
            nc.scalar.activation(out=fac[:, i:i + 1], in_=rcp[:, i:i + 1], func=ACT.Identity, scale=448.0)

        def new_byte_tile(i):
            o_t = xs.tile([P, EMBED], FP8, name="o8")
            byte_tiles[i] = o_t
            return o_t

        def cast_on_scalar(i):
            nc.scalar.activation(out=new_byte_tile(i)[:, 0:EMBED], in_=x_tiles[i][:, 0:EMBED], func=ACT.Identity,
                                 scale=fac[:, i:i + 1], bias=zeros[:, 0:1], saturate=False)


        def quantize_w(h):
            nc.vector.quantize_mx(out=wc[:, h * HALF:(h + 1) * HALF].bitcast(FP8X4),
                                  scales=ws[:, h * HALF:(h + 1) * HALF],
                                  in_=gw[:, h * 1024:(h + 1) * 1024].bitcast(BF16))

        def quantize_video(e):
            nc.vector.quantize_mx(out=vc[:, e * 256:(e + 1) * 256].bitcast(FP8X4),
                                  scales=vs[:, e * 256:(e + 1) * 256],
                                  in_=gv[:, e * 576:e * 576 + 512].bitcast(BF16))

        def quantize_last_tile():
            nc.vector.quantize_mx(out=vc[:, 1024:1152].bitcast(FP8X4), scales=vs[:, 1024:1152],
                                  in_=g2[:].bitcast(BF16))

        def pos_plus_b_on_vector(h):
            nc.vector.tensor_tensor(out=posb[h][:, 0:HALF], in0=banks[("b", 0)][:], in1=pos_sb[h][:, 0:HALF],
                                    op=ALU.add)

        def x_of(i):
            if i not in x_tiles:
                x_t = xs.tile([P, EMBED], F32, name="x")
                x_tiles[i] = x_t
            return x_tiles[i]

        def add_on_vector(i, n):
            sl = slice(n * HALF, (n + 1) * HALF)
            nc.vector.tensor_tensor(out=x_of(i)[:, sl], in0=banks[("a", i, n)][:],
                                    in1=posb[TILES[i][1]][:, sl], op=ALU.add)

        def row_max(i):
            nc.vector.tensor_reduce(out=amax[:, i:i + 1], in_=x_tiles[i][:], axis=AX.X, op=ALU.max,
                                    apply_absolute_value=True)

        def reciprocal(i):
            nc.vector.reciprocal(out=rcp[:, i:i + 1], in_=amax[:, i:i + 1])

        def factor_on_vector(i):
            nc.vector.tensor_scalar(out=fac[:, i:i + 1], in0=rcp[:, i:i + 1], scalar1=448.0,
                                    scalar2=None, op0=ALU.mult)

        def cast_on_vector(i):
            nc.vector.tensor_scalar(out=new_byte_tile(i)[:, 0:EMBED], in0=x_tiles[i][:, 0:EMBED],
                                    scalar1=fac[:, i:i + 1], scalar2=None, op0=ALU.mult,
                                    saturate=False)


        def pos_plus_b_on_gpsimd(h):
            nc.gpsimd.tensor_tensor(out=posb[h][:, HALF:EMBED], in0=pos_sb[h][:, HALF:EMBED],
                                    in1=bbt[:, HALF:EMBED], op=ALU.add)

        def add_on_gpsimd(i):
            nc.gpsimd.tensor_tensor(out=x_of(i)[:, HALF:EMBED], in0=y_tiles[i][:],
                                    in1=posb[TILES[i][1]][:, HALF:EMBED], op=ALU.add)


        def store_x(i, n):
            e, h = TILES[i]
            sl = slice(n * HALF, (n + 1) * HALF)
            if h == 2:
                nc.sync.dma_start(out=out_0[:, 256:288, sl].rearrange("b n e -> n b e"), in_=x_tiles[i][:, sl])
            else:
                nc.sync.dma_start(out=out_0[e, h * P:(h + 1) * P, sl], in_=x_tiles[i][:, sl])

        def store_bytes(i):
            e, h = TILES[i]
            if h == 2:
                dst = out_1[:, 256:288, :].rearrange("b n e -> n b e")
            else:
                dst = out_1[e, h * P:(h + 1) * P, :]
            nc.sync.dma_start(out=dst, in_=byte_tiles[i][:].bitcast(U8))

        nc.gpsimd.memset(brow[:].bitcast(F32), 0.0)
        nc.gpsimd.memset(dmy[:], 0.0)
        nc.vector.memset(zeros[:], 0.0)
        nc.vector.memset(relaid[0][ROWS:P, :], 0.0)
        make_identity(nc, idn[:])
        nc.gpsimd.memset(one[:], 1.0)
        load_w(0)
        load_video(0, 0)
        load_b()
        load_video(0, 1)
        load_pos(0)
        nc.scalar.activation(out=wrm[:], in_=zeros[:], func=ACT.Identity)
        load_pos(1)
        load_w(1)
        load_pos(2)
        load_video(1, 0)
        load_video(1, 1)
        nc.vector.memset(relaid[1][ROWS:P, :], 0.0)

        with tc.manual_schedule():
            for k in range(5):
                keep_pe_busy()
            transpose_w(0)
            transpose_w(1)
            keep_pe_busy()
            spread_b()
            keep_pe_busy()
            copy_w(0)
            copy_w(1)
            copy_b_for_gpsimd()
            for jp in range(3):
                reorder_on_vector(0, jp)
            quantize_w(0)
            for h in range(3):
                pos_plus_b_on_gpsimd(h)
            transpose_video(0, 0)
            transpose_video(0, 1)
            keep_pe_busy()
            transpose_video(0, 2)
            transpose_w(2)
            keep_pe_busy()
            transpose_w(3)
            for jp in range(3):
                copy_video(0, jp)
            pos_plus_b_on_vector(0)
            pos_plus_b_on_vector(1)
            quantize_video(0)
            quantize_video(1)
            pos_plus_b_on_vector(2)
            for i in range(4):
                mx_pass(i, 0)
            copy_w(2)
            copy_w(3)
            quantize_w(1)
            add_on_vector(0, 0)
            store_x(0, 0)
            for jp in range(3):
                reorder_on_scalar(1, jp)
            add_on_vector(1, 0)
            store_x(1, 0)
            mx_pass(0, 1)
            mx_pass(1, 1)
            for jp in range(3):
                transpose_video(1, jp)
            mx_pass(2, 1)
            mx_pass(3, 1)
            copy_second_bank(1)
            add_on_gpsimd(1)
            add_on_vector(2, 0)
            store_x(2, 0)
            add_on_vector(0, 1)
            store_x(0, 1)
            add_on_vector(3, 0)
            store_x(3, 0)
            for jp in range(3):
                copy_video(1, jp)
            gather_last_tile()
            row_max(0)
            quantize_video(2)
            quantize_video(3)
            quantize_last_tile()
            reciprocal(0)
            store_x(1, 1)
            for i in (2, 3):
                copy_second_bank(i)
                add_on_gpsimd(i)
            factor_on_scalar(0)
            cast_on_scalar(0)
            store_bytes(0)
            mx_pass(4, 0)
            mx_pass(4, 1)
            copy_second_ahead = 4
            add_first_ahead = 3
            for i in range(1, LAST):
                if i + copy_second_ahead <= LAST:
                    mx_pass(i + copy_second_ahead, 0)
                    mx_pass(i + copy_second_ahead, 1)
                row_max(i)
                if i + add_first_ahead <= LAST:
                    add_on_vector(i + add_first_ahead, 0)
                    store_x(i + add_first_ahead, 0)
                reciprocal(i)
                store_x(i + 1, 1)
                if i == 1:
                    copy_second_bank(4)
                    add_on_gpsimd(4)
                factor_on_scalar(i)
                if i + copy_second_ahead <= LAST:
                    copy_second_bank(i + copy_second_ahead)
                    add_on_gpsimd(i + copy_second_ahead)
                cast_on_scalar(i)
                store_bytes(i)
            row_max(LAST)
            reciprocal(LAST)
            factor_on_vector(LAST)
            cast_on_vector(LAST)
            store_bytes(LAST)
